import numpy as np
import ml_dtypes


def mxq(x, axis, fmt="e4m3"):
    dtype, down = {"e4m3": (ml_dtypes.float8_e4m3fn, 7), "e5m2": (ml_dtypes.float8_e5m2, 14)}[fmt]
    v = np.moveaxis(np.asarray(x, np.float32).astype(ml_dtypes.bfloat16).astype(np.float64), axis, -1)
    blocks = v.reshape(v.shape[:-1] + (-1, 32))
    amax = np.abs(blocks).max(-1, keepdims=True)
    byte = np.maximum(np.where(amax > 0, np.frexp(amax)[1] - 1 + 127, 0) - down, 1)
    scale = np.exp2(byte - 127.0)
    codes = (blocks / scale).astype(np.float32).astype(dtype).astype(np.float64)
    return np.moveaxis((codes * scale).reshape(v.shape), -1, axis)


BF16 = ml_dtypes.bfloat16


def bf(x):
    return np.asarray(x, np.float32).astype(BF16)


def f64(x):
    return np.asarray(x).astype(np.float64)


B, I, O, G, P = 16384, 128, 512, 2, 2
L = G + P
SCALE_SPLINE = 1.0


def setup_inputs():
    x = np.random.uniform(-1.0, 1.0, (B, I))
    sw = np.random.standard_normal((O, I, L)) * 2.0 / np.sqrt(I)
    bw = np.random.standard_normal((O, I)) * 1.0 / np.sqrt(I)
    g = np.random.standard_normal((B, O)) * np.exp2(np.random.randint(-12, 1, (B, 1))) * 0.25
    return {"x": bf(x),
            "base_weight": bf(bw),
            "spline_weight": bf(sw),
            "grid": bf(np.arange(-P, G + P + 1) * (2.0 / G) - 1.0),
            "grad_out": bf(g)}


def b_spline_basis(x, grid, k):
    xe = x[..., None]
    basis = ((xe >= grid[:-1]) & (xe < grid[1:])).astype(np.float64)
    for d in range(1, k + 1):
        left_denom = grid[d:-1] - grid[:-(d + 1)]
        right_denom = grid[d + 1:] - grid[1:-d]
        left_denom = np.where(left_denom > 0, left_denom, 1.0)
        right_denom = np.where(right_denom > 0, right_denom, 1.0)
        basis = ((xe - grid[:-(d + 1)]) / left_denom * basis[..., :-1]
                 + (grid[d + 1:] - xe) / right_denom * basis[..., 1:])
    return basis


def reference(x, base_weight, spline_weight, grid, grad_out):
    x, grid, g = f64(x), f64(grid), f64(grad_out)
    basis2d = b_spline_basis(x, grid, P).reshape(B, I * L)
    gw = mxq(g, 0, "e5m2").T @ mxq(basis2d, 0, "e4m3")
    return (SCALE_SPLINE * gw).reshape(O, I, L)

@@ -1,0 +1,121 @@
+from contextlib import ExitStack
+
+import concourse.mybir as mybir
+
+BF16 = mybir.dt.bfloat16
+F32 = mybir.dt.float32
+U32 = mybir.dt.uint32
+U8 = mybir.dt.uint8
+E4M3_X4 = mybir.dt.float8_e4m3fn_x4
+E5M2_X4 = mybir.dt.float8_e5m2_x4
+ALU = mybir.AluOpType
+ACT = mybir.ActivationFunctionType
+
+TOKENS, FEATURES, OUTS, SPLINES = 16384, 128, 512, 4
+P = 128
+PACK = 4
+K_PASS = P * PACK
+CHUNK = 2
+N_CHUNKS = TOKENS // (K_PASS * CHUNK)
+COLS = FEATURES * SPLINES
+O_BLOCKS = OUTS // P
+RUN = 4
+
+G_COLS_VECTOR = 160
+
+FLOPS = 2 * TOKENS * OUTS * COLS
+BYTES = TOKENS * FEATURES * 2 + TOKENS * OUTS * 2 + OUTS * COLS * 4
+
+
+def group_tokens(copy, grouped, rows):
+    copy(
+        out=grouped.rearrange("p (q r) t -> p q t r", r=RUN),
+        in_=rows.rearrange("p t (q r) -> p q t r", r=RUN),
+    )
+
+
+def tile_kanlayer_t_kernel(tc, x, base_weight, spline_weight, grid, grad_out, out):
+    nc = tc.nc
+    x_chunks = x.rearrange("(n c p t) i -> n p c (t i)", c=CHUNK, p=P, t=PACK)
+    g_chunks = grad_out.rearrange("(n c p t) o -> n p c (t o)", c=CHUNK, p=P, t=PACK)
+
+    with ExitStack() as stack:
+        loads = stack.enter_context(tc.tile_pool(name="loads", bufs=4))
+        work = stack.enter_context(tc.tile_pool(name="work", bufs=3))
+        packed = stack.enter_context(tc.tile_pool(name="packed", bufs=3))
+        results = stack.enter_context(tc.tile_pool(name="results", bufs=2))
+        psum = stack.enter_context(tc.psum_pool(name="psum", bufs=1))
+
+        sums = [psum.tile([P, COLS], F32, name="sums%d" % ob) for ob in range(O_BLOCKS)]
+
+        for n in range(N_CHUNKS):
+            x_rows = loads.tile([P, CHUNK, PACK, FEATURES], BF16)
+            nc.sync.dma_start(out=x_rows[:].rearrange("p c t i -> p c (t i)"), in_=x_chunks[n])
+            g_rows = loads.tile([P, CHUNK, PACK, OUTS], BF16)
+            nc.sync.dma_start(out=g_rows[:].rearrange("p c t o -> p c (t o)"), in_=g_chunks[n])
+
+            v = work.tile([P, CHUNK, FEATURES, PACK], BF16)
+            for c in range(CHUNK):
+                group_tokens(nc.vector.tensor_copy, v[:, c], x_rows[:, c])
+            v_flat = v[:].rearrange("p c i t -> p c (i t)")
+
+            part = work.tile([P, CHUNK, 2, FEATURES * PACK], BF16)
+            nc.vector.tensor_scalar_min(out=part[:, :, 0, :], in0=v_flat, scalar1=0.0)
+            nc.vector.tensor_scalar_max(out=part[:, :, 1, :], in0=v_flat, scalar1=0.0)
+            part_sq = work.tile([P, CHUNK, 2, FEATURES * PACK], F32)
+            nc.scalar.activation(out=part_sq[:], in_=part[:], func=ACT.Square)
+            far_sq = work.tile([P, CHUNK, 2, FEATURES * PACK], F32)
+            nc.scalar.activation(out=far_sq[:, :, 0, :], in_=v_flat, func=ACT.Square, bias=1.0, scale=-1.0)
+            nc.scalar.activation(out=far_sq[:, :, 1, :], in_=v_flat, func=ACT.Square, bias=1.0, scale=1.0)
+
+            basis2 = work.tile([P, CHUNK, SPLINES, FEATURES * PACK], BF16, align_bytes=64)
+            nc.vector.tensor_copy(out=basis2[:, :, 0 : SPLINES : SPLINES - 1, :], in_=part_sq[:])
+            nc.vector.scalar_tensor_tensor(
+                out=basis2[:, :, 1:3, :].rearrange("p c l w -> p c (l w)"),
+                in0=part_sq[:].rearrange("p c s w -> p c (s w)"),
+                scalar=-3.0,
+                in1=far_sq[:].rearrange("p c s w -> p c (s w)"),
+                op0=ALU.mult,
+                op1=ALU.add,
+            )
+            b_codes = packed.tile([P, CHUNK, COLS], U32, align_bytes=64)
+            b_scales = packed.tile([P, CHUNK, COLS], U8, align_bytes=64)
+            nc.vector.quantize_mx(
+                out=b_codes[:].rearrange("p c w -> p (c w)").bitcast(E4M3_X4),
+                scales=b_scales[:].rearrange("p c w -> p (c w)"),
+                in_=basis2[:].rearrange("p c l w -> p (c l w)"),
+            )
+
+            g = work.tile([P, CHUNK, OUTS, PACK], BF16, align_bytes=64)
+            for c in range(CHUNK):
+                group_tokens(nc.vector.tensor_copy, g[:, c, :G_COLS_VECTOR, :], g_rows[:, c, :, :G_COLS_VECTOR])
+                group_tokens(nc.scalar.copy, g[:, c, G_COLS_VECTOR:, :], g_rows[:, c, :, G_COLS_VECTOR:])
+            g_codes = packed.tile([P, CHUNK, OUTS], U32, align_bytes=64)
+            g_scales = packed.tile([P, CHUNK, OUTS], U8, align_bytes=64)
+            nc.vector.quantize_mx(
+                out=g_codes[:].rearrange("p c o -> p (c o)").bitcast(E5M2_X4),
+                scales=g_scales[:].rearrange("p c o -> p (c o)"),
+                in_=g[:].rearrange("p c o t -> p (c o t)"),
+            )
+
+            for c in range(CHUNK):
+                for ob in range(O_BLOCKS):
+                    o_cols = slice(ob * P, (ob + 1) * P)
+                    nc.tensor.matmul_mx(
+                        out=sums[ob][:],
+                        lhsT=g_codes[:, c, o_cols].bitcast(E5M2_X4),
+                        lhsT_scale=g_scales[:, c, o_cols],
+                        rhs=b_codes[:, c, :].bitcast(E4M3_X4),
+                        rhs_scale=b_scales[:, c, :],
+                        start=(n == 0 and c == 0),
+                        stop=(n == N_CHUNKS - 1 and c == CHUNK - 1),
+                    )
+
+        for ob in range(O_BLOCKS):
+            result = results.tile([P, FEATURES, SPLINES], F32)
+            columns = sums[ob][:].rearrange("p (l i) -> p i l", l=SPLINES)
+            if ob % 2 == 0:
+                nc.vector.tensor_scalar_mul(out=result[:], in0=columns, scalar1=0.5)
+            else:
+                nc.scalar.mul(out=result[:], in_=columns, mul=0.5)
+            nc.sync.dma_start(out=out[ob * P : (ob + 1) * P], in_=result[:])

@@ -1,5 +1,6 @@
 from contextlib import ExitStack
 
+import concourse.masks as masks
 import concourse.mybir as mybir
 
 BF16 = mybir.dt.bfloat16
@@ -21,31 +22,32 @@ COLS = FEATURES * SPLINES
 O_BLOCKS = OUTS // P
 RUN = 4
 
-G_COLS_VECTOR = 160
+G_COLS_VECTOR = 88
+G_COLS_TENSOR = 192
 
 FLOPS = 2 * TOKENS * OUTS * COLS
 BYTES = TOKENS * FEATURES * 2 + TOKENS * OUTS * 2 + OUTS * COLS * 4
-
-
-def group_tokens(copy, grouped, rows):
-    copy(
-        out=grouped.rearrange("p (q r) t -> p q t r", r=RUN),
-        in_=rows.rearrange("p t (q r) -> p q t r", r=RUN),
-    )
 
 
 def tile_kanlayer_t_kernel(tc, x, base_weight, spline_weight, grid, grad_out, out):
     nc = tc.nc
     x_chunks = x.rearrange("(n c p t) i -> n p c (t i)", c=CHUNK, p=P, t=PACK)
     g_chunks = grad_out.rearrange("(n c p t) o -> n p c (t o)", c=CHUNK, p=P, t=PACK)
+    vector_cols = slice(0, G_COLS_VECTOR)
+    tensor_cols = slice(G_COLS_VECTOR, G_COLS_VECTOR + G_COLS_TENSOR)
+    scalar_cols = slice(G_COLS_VECTOR + G_COLS_TENSOR, OUTS)
 
     with ExitStack() as stack:
+        consts = stack.enter_context(tc.tile_pool(name="consts", bufs=1))
         loads = stack.enter_context(tc.tile_pool(name="loads", bufs=4))
         work = stack.enter_context(tc.tile_pool(name="work", bufs=3))
         packed = stack.enter_context(tc.tile_pool(name="packed", bufs=3))
         results = stack.enter_context(tc.tile_pool(name="results", bufs=2))
         psum = stack.enter_context(tc.psum_pool(name="psum", bufs=1))
+        psum_g = stack.enter_context(tc.psum_pool(name="psum_g", bufs=4))
 
+        identity = consts.tile([P, P], BF16)
+        masks.make_identity(nc, identity[:])
         sums = [psum.tile([P, COLS], F32, name="sums%d" % ob) for ob in range(O_BLOCKS)]
 
         for n in range(N_CHUNKS):
@@ -55,10 +57,11 @@ def tile_kanlayer_t_kernel(tc, x, base_weight, spline_weight, grid, grad_out, ou
             nc.sync.dma_start(out=g_rows[:].rearrange("p c t o -> p c (t o)"), in_=g_chunks[n])
 
             v = work.tile([P, CHUNK, FEATURES, PACK], BF16)
-            for c in range(CHUNK):
-                group_tokens(nc.vector.tensor_copy, v[:, c], x_rows[:, c])
+            nc.vector.tensor_copy(
+                out=v[:].rearrange("p c (q r) t -> p c q t r", r=RUN),
+                in_=x_rows[:].rearrange("p c t (q r) -> p c q t r", r=RUN),
+            )
             v_flat = v[:].rearrange("p c i t -> p c (i t)")
-
             part = work.tile([P, CHUNK, 2, FEATURES * PACK], BF16)
             nc.vector.tensor_scalar_min(out=part[:, :, 0, :], in0=v_flat, scalar1=0.0)
             nc.vector.tensor_scalar_max(out=part[:, :, 1, :], in0=v_flat, scalar1=0.0)
@@ -87,9 +90,26 @@ def tile_kanlayer_t_kernel(tc, x, base_weight, spline_weight, grid, grad_out, ou
             )
 
             g = work.tile([P, CHUNK, OUTS, PACK], BF16, align_bytes=64)
+            nc.vector.tensor_copy(
+                out=g[:, :, vector_cols, :].rearrange("p c (q r) t -> p c q t r", r=RUN),
+                in_=g_rows[:, :, :, vector_cols].rearrange("p c t (q r) -> p c q t r", r=RUN),
+            )
             for c in range(CHUNK):
-                group_tokens(nc.vector.tensor_copy, g[:, c, :G_COLS_VECTOR, :], g_rows[:, c, :, :G_COLS_VECTOR])
-                group_tokens(nc.scalar.copy, g[:, c, G_COLS_VECTOR:, :], g_rows[:, c, :, G_COLS_VECTOR:])
+                passed = psum_g.tile([P, G_COLS_TENSOR, PACK], BF16)
+                for half in range(2):
+                    half_cols = slice(half * G_COLS_TENSOR // 2, (half + 1) * G_COLS_TENSOR // 2)
+                    nc.tensor.matmul(
+                        out=passed[:, half_cols, :].rearrange("p o t -> p t o"),
+                        lhsT=identity[:],
+                        rhs=g_rows[:, c, :, tensor_cols][:, :, half_cols],
+                        start=True,
+                        stop=True,
+                    )
+                nc.scalar.copy(out=g[:, c, tensor_cols, :], in_=passed[:])
+                nc.scalar.copy(
+                    out=g[:, c, scalar_cols, :].rearrange("p (q r) t -> p q t r", r=RUN),
+                    in_=g_rows[:, c, :, scalar_cols].rearrange("p t (q r) -> p q t r", r=RUN),
+                )
             g_codes = packed.tile([P, CHUNK, OUTS], U32, align_bytes=64)
             g_scales = packed.tile([P, CHUNK, OUTS], U8, align_bytes=64)
             nc.vector.quantize_mx(

@@ -40,9 +40,11 @@ def tile_kanlayer_t_kernel(tc, x, base_weight, spline_weight, grid, grad_out, ou
     with ExitStack() as stack:
         consts = stack.enter_context(tc.tile_pool(name="consts", bufs=1))
         loads = stack.enter_context(tc.tile_pool(name="loads", bufs=4))
-        work = stack.enter_context(tc.tile_pool(name="work", bufs=3))
+        split = stack.enter_context(tc.tile_pool(name="split", bufs=3))
+        squares = stack.enter_context(tc.tile_pool(name="squares", bufs=3))
+        ready = stack.enter_context(tc.tile_pool(name="ready", bufs=3))
         packed = stack.enter_context(tc.tile_pool(name="packed", bufs=3))
-        results = stack.enter_context(tc.tile_pool(name="results", bufs=2))
+        results = stack.enter_context(tc.tile_pool(name="results", bufs=4))
         psum = stack.enter_context(tc.psum_pool(name="psum", bufs=1))
         psum_g = stack.enter_context(tc.psum_pool(name="psum_g", bufs=4))
 
@@ -50,50 +52,42 @@ def tile_kanlayer_t_kernel(tc, x, base_weight, spline_weight, grid, grad_out, ou
         masks.make_identity(nc, identity[:])
         sums = [psum.tile([P, COLS], F32, name="sums%d" % ob) for ob in range(O_BLOCKS)]
 
-        for n in range(N_CHUNKS):
+        stack.enter_context(tc.manual_schedule())
+        held = {}
+
+        def load(n):
             x_rows = loads.tile([P, CHUNK, PACK, FEATURES], BF16)
             nc.sync.dma_start(out=x_rows[:].rearrange("p c t i -> p c (t i)"), in_=x_chunks[n])
             g_rows = loads.tile([P, CHUNK, PACK, OUTS], BF16)
             nc.sync.dma_start(out=g_rows[:].rearrange("p c t o -> p c (t o)"), in_=g_chunks[n])
+            held[("x_rows", n)] = x_rows
+            held[("g_rows", n)] = g_rows
 
-            v = work.tile([P, CHUNK, FEATURES, PACK], BF16)
+        def vector_regroup_x(n):
+            v = split.tile([P, CHUNK, FEATURES, PACK], BF16)
             nc.vector.tensor_copy(
                 out=v[:].rearrange("p c (q r) t -> p c q t r", r=RUN),
-                in_=x_rows[:].rearrange("p c t (q r) -> p c q t r", r=RUN),
+                in_=held[("x_rows", n)][:].rearrange("p c t (q r) -> p c q t r", r=RUN),
             )
-            v_flat = v[:].rearrange("p c i t -> p c (i t)")
-            part = work.tile([P, CHUNK, 2, FEATURES * PACK], BF16)
+            held[("v", n)] = v
+
+        def vector_clamp(n):
+            v_flat = held[("v", n)][:].rearrange("p c i t -> p c (i t)")
+            part = split.tile([P, CHUNK, 2, FEATURES * PACK], BF16)
             nc.vector.tensor_scalar_min(out=part[:, :, 0, :], in0=v_flat, scalar1=0.0)
             nc.vector.tensor_scalar_max(out=part[:, :, 1, :], in0=v_flat, scalar1=0.0)
-            part_sq = work.tile([P, CHUNK, 2, FEATURES * PACK], F32)
-            nc.scalar.activation(out=part_sq[:], in_=part[:], func=ACT.Square)
-            far_sq = work.tile([P, CHUNK, 2, FEATURES * PACK], F32)
-            nc.scalar.activation(out=far_sq[:, :, 0, :], in_=v_flat, func=ACT.Square, bias=1.0, scale=-1.0)
-            nc.scalar.activation(out=far_sq[:, :, 1, :], in_=v_flat, func=ACT.Square, bias=1.0, scale=1.0)
+            held[("part", n)] = part
 
-            basis2 = work.tile([P, CHUNK, SPLINES, FEATURES * PACK], BF16, align_bytes=64)
-            nc.vector.tensor_copy(out=basis2[:, :, 0 : SPLINES : SPLINES - 1, :], in_=part_sq[:])
-            nc.vector.scalar_tensor_tensor(
-                out=basis2[:, :, 1:3, :].rearrange("p c l w -> p c (l w)"),
-                in0=part_sq[:].rearrange("p c s w -> p c (s w)"),
-                scalar=-3.0,
-                in1=far_sq[:].rearrange("p c s w -> p c (s w)"),
-                op0=ALU.mult,
-                op1=ALU.add,
-            )
-            b_codes = packed.tile([P, CHUNK, COLS], U32, align_bytes=64)
-            b_scales = packed.tile([P, CHUNK, COLS], U8, align_bytes=64)
-            nc.vector.quantize_mx(
-                out=b_codes[:].rearrange("p c w -> p (c w)").bitcast(E4M3_X4),
-                scales=b_scales[:].rearrange("p c w -> p (c w)"),
-                in_=basis2[:].rearrange("p c l w -> p (c l w)"),
-            )
-
-            g = work.tile([P, CHUNK, OUTS, PACK], BF16, align_bytes=64)
+        def vector_regroup_g(n):
+            g = ready.tile([P, CHUNK, OUTS, PACK], BF16, align_bytes=64)
             nc.vector.tensor_copy(
                 out=g[:, :, vector_cols, :].rearrange("p c (q r) t -> p c q t r", r=RUN),
-                in_=g_rows[:, :, :, vector_cols].rearrange("p c t (q r) -> p c q t r", r=RUN),
+                in_=held[("g_rows", n)][:, :, :, vector_cols].rearrange("p c t (q r) -> p c q t r", r=RUN),
             )
+            held[("g", n)] = g
+
+        def tensor_pass_g(n):
+            g_rows = held[("g_rows", n)]
             for c in range(CHUNK):
                 passed = psum_g.tile([P, G_COLS_TENSOR, PACK], BF16)
                 for half in range(2):
@@ -105,31 +99,108 @@ def tile_kanlayer_t_kernel(tc, x, base_weight, spline_weight, grid, grad_out, ou
                         start=True,
                         stop=True,
                     )
-                nc.scalar.copy(out=g[:, c, tensor_cols, :], in_=passed[:])
+                held[("passed", n, c)] = passed
+
+        def scalar_work(n):
+            v_flat = held[("v", n)][:].rearrange("p c i t -> p c (i t)")
+            far_sq = squares.tile([P, CHUNK, 2, FEATURES * PACK], F32)
+            nc.scalar.activation(out=far_sq[:, :, 0, :], in_=v_flat, func=ACT.Square, bias=1.0, scale=-1.0)
+            nc.scalar.activation(out=far_sq[:, :, 1, :], in_=v_flat, func=ACT.Square, bias=1.0, scale=1.0)
+            part_sq = squares.tile([P, CHUNK, 2, FEATURES * PACK], F32)
+            nc.scalar.activation(out=part_sq[:], in_=held[("part", n)][:], func=ACT.Square)
+            held[("far_sq", n)] = far_sq
+            held[("part_sq", n)] = part_sq
+            g = held[("g", n)]
+            g_rows = held[("g_rows", n)]
+            for c in range(CHUNK):
+                nc.scalar.copy(out=g[:, c, tensor_cols, :], in_=held[("passed", n, c)][:])
                 nc.scalar.copy(
                     out=g[:, c, scalar_cols, :].rearrange("p (q r) t -> p q t r", r=RUN),
                     in_=g_rows[:, c, :, scalar_cols].rearrange("p t (q r) -> p q t r", r=RUN),
                 )
+
+        def vector_inner(n):
+            basis2 = ready.tile([P, CHUNK, SPLINES, FEATURES * PACK], BF16, align_bytes=64)
+            nc.vector.scalar_tensor_tensor(
+                out=basis2[:, :, 1:3, :].rearrange("p c l w -> p c (l w)"),
+                in0=held[("part_sq", n)][:].rearrange("p c s w -> p c (s w)"),
+                scalar=-3.0,
+                in1=held[("far_sq", n)][:].rearrange("p c s w -> p c (s w)"),
+                op0=ALU.mult,
+                op1=ALU.add,
+            )
+            held[("basis2", n)] = basis2
+
+        def vector_outer(n):
+            nc.vector.tensor_copy(
+                out=held[("basis2", n)][:, :, 0 : SPLINES : SPLINES - 1, :], in_=held[("part_sq", n)][:]
+            )
+
+        def quantize_basis(n):
+            b_codes = packed.tile([P, CHUNK, COLS], U32, align_bytes=64)
+            b_scales = packed.tile([P, CHUNK, COLS], U8, align_bytes=64)
+            nc.vector.quantize_mx(
+                out=b_codes[:].rearrange("p c w -> p (c w)").bitcast(E4M3_X4),
+                scales=b_scales[:].rearrange("p c w -> p (c w)"),
+                in_=held[("basis2", n)][:].rearrange("p c l w -> p (c l w)"),
+            )
+            held[("b_codes", n)] = b_codes
+            held[("b_scales", n)] = b_scales
+
+        def quantize_g(n):
             g_codes = packed.tile([P, CHUNK, OUTS], U32, align_bytes=64)
             g_scales = packed.tile([P, CHUNK, OUTS], U8, align_bytes=64)
             nc.vector.quantize_mx(
                 out=g_codes[:].rearrange("p c o -> p (c o)").bitcast(E5M2_X4),
                 scales=g_scales[:].rearrange("p c o -> p (c o)"),
-                in_=g[:].rearrange("p c o t -> p (c o t)"),
+                in_=held[("g", n)][:].rearrange("p c o t -> p (c o t)"),
             )
+            held[("g_codes", n)] = g_codes
+            held[("g_scales", n)] = g_scales
 
-            for c in range(CHUNK):
-                for ob in range(O_BLOCKS):
-                    o_cols = slice(ob * P, (ob + 1) * P)
-                    nc.tensor.matmul_mx(
-                        out=sums[ob][:],
-                        lhsT=g_codes[:, c, o_cols].bitcast(E5M2_X4),
-                        lhsT_scale=g_scales[:, c, o_cols],
-                        rhs=b_codes[:, c, :].bitcast(E4M3_X4),
-                        rhs_scale=b_scales[:, c, :],
-                        start=(n == 0 and c == 0),
-                        stop=(n == N_CHUNKS - 1 and c == CHUNK - 1),
-                    )
+        def multiply(n):
+            last = n == N_CHUNKS - 1
+            order = [(c, ob) for c in range(CHUNK) for ob in range(O_BLOCKS)]
+            if last:
+                order = [(c, ob) for ob in range(O_BLOCKS) for c in range(CHUNK)]
+            for c, ob in order:
+                o_cols = slice(ob * P, (ob + 1) * P)
+                nc.tensor.matmul_mx(
+                    out=sums[ob][:],
+                    lhsT=held[("g_codes", n)][:, c, o_cols].bitcast(E5M2_X4),
+                    lhsT_scale=held[("g_scales", n)][:, c, o_cols],
+                    rhs=held[("b_codes", n)][:, c, :].bitcast(E4M3_X4),
+                    rhs_scale=held[("b_scales", n)][:, c, :],
+                    start=(n == 0 and c == 0),
+                    stop=(last and c == CHUNK - 1),
+                )
+
+        def valid(n):
+            return 0 <= n < N_CHUNKS
+
+        for n in range(-3, N_CHUNKS):
+            if valid(n + 3):
+                load(n + 3)
+            if valid(n):
+                vector_inner(n)
+            if valid(n + 2):
+                vector_regroup_x(n + 2)
+            if valid(n):
+                vector_outer(n)
+            if valid(n + 2):
+                vector_clamp(n + 2)
+            if valid(n):
+                quantize_basis(n)
+            if valid(n + 1):
+                vector_regroup_g(n + 1)
+            if valid(n):
+                quantize_g(n)
+            if valid(n + 2):
+                tensor_pass_g(n + 2)
+            if valid(n + 1):
+                scalar_work(n + 1)
+            if valid(n):
+                multiply(n)
 
         for ob in range(O_BLOCKS):
             result = results.tile([P, FEATURES, SPLINES], F32)

@@ -22,8 +22,8 @@ COLS = FEATURES * SPLINES
 O_BLOCKS = OUTS // P
 RUN = 4
 
-G_COLS_VECTOR = 88
-G_COLS_TENSOR = 192
+G_COLS_VECTOR = 76
+G_COLS_TENSOR = 204
 
 FLOPS = 2 * TOKENS * OUTS * COLS
 BYTES = TOKENS * FEATURES * 2 + TOKENS * OUTS * 2 + OUTS * COLS * 4
@@ -64,18 +64,20 @@ def tile_kanlayer_t_kernel(tc, x, base_weight, spline_weight, grid, grad_out, ou
             held[("g_rows", n)] = g_rows
 
         def vector_regroup_x(n):
-            v = split.tile([P, CHUNK, FEATURES, PACK], BF16)
+            signed = split.tile([P, CHUNK, 2, FEATURES * PACK], BF16)
             nc.vector.tensor_copy(
-                out=v[:].rearrange("p c (q r) t -> p c q t r", r=RUN),
+                out=signed[:, :, 1, :].rearrange("p c (q r t) -> p c q t r", r=RUN, t=PACK),
                 in_=held[("x_rows", n)][:].rearrange("p c t (q r) -> p c q t r", r=RUN),
             )
-            held[("v", n)] = v
+            held[("signed", n)] = signed
+
+        def vector_negate(n):
+            signed = held[("signed", n)]
+            nc.vector.tensor_scalar_mul(out=signed[:, :, 0, :], in0=signed[:, :, 1, :], scalar1=-1.0)
 
         def vector_clamp(n):
-            v_flat = held[("v", n)][:].rearrange("p c i t -> p c (i t)")
             part = split.tile([P, CHUNK, 2, FEATURES * PACK], BF16)
-            nc.vector.tensor_scalar_min(out=part[:, :, 0, :], in0=v_flat, scalar1=0.0)
-            nc.vector.tensor_scalar_max(out=part[:, :, 1, :], in0=v_flat, scalar1=0.0)
+            nc.vector.tensor_scalar_max(out=part[:], in0=held[("signed", n)][:], scalar1=0.0)
             held[("part", n)] = part
 
         def vector_regroup_g(n):
@@ -102,10 +104,8 @@ def tile_kanlayer_t_kernel(tc, x, base_weight, spline_weight, grid, grad_out, ou
                 held[("passed", n, c)] = passed
 
         def scalar_work(n):
-            v_flat = held[("v", n)][:].rearrange("p c i t -> p c (i t)")
             far_sq = squares.tile([P, CHUNK, 2, FEATURES * PACK], F32)
-            nc.scalar.activation(out=far_sq[:, :, 0, :], in_=v_flat, func=ACT.Square, bias=1.0, scale=-1.0)
-            nc.scalar.activation(out=far_sq[:, :, 1, :], in_=v_flat, func=ACT.Square, bias=1.0, scale=1.0)
+            nc.scalar.activation(out=far_sq[:], in_=held[("signed", n)][:], func=ACT.Square, bias=1.0, scale=1.0)
             part_sq = squares.tile([P, CHUNK, 2, FEATURES * PACK], F32)
             nc.scalar.activation(out=part_sq[:], in_=held[("part", n)][:], func=ACT.Square)
             held[("far_sq", n)] = far_sq
@@ -114,10 +114,10 @@ def tile_kanlayer_t_kernel(tc, x, base_weight, spline_weight, grid, grad_out, ou
             g_rows = held[("g_rows", n)]
             for c in range(CHUNK):
                 nc.scalar.copy(out=g[:, c, tensor_cols, :], in_=held[("passed", n, c)][:])
-                nc.scalar.copy(
-                    out=g[:, c, scalar_cols, :].rearrange("p (q r) t -> p q t r", r=RUN),
-                    in_=g_rows[:, c, :, scalar_cols].rearrange("p t (q r) -> p q t r", r=RUN),
-                )
+            nc.scalar.copy(
+                out=g[:, :, scalar_cols, :].rearrange("p c (q r) t -> p c q t r", r=RUN),
+                in_=g_rows[:, :, :, scalar_cols].rearrange("p c t (q r) -> p c q t r", r=RUN),
+            )
 
         def vector_inner(n):
             basis2 = ready.tile([P, CHUNK, SPLINES, FEATURES * PACK], BF16, align_bytes=64)
@@ -181,20 +181,20 @@ def tile_kanlayer_t_kernel(tc, x, base_weight, spline_weight, grid, grad_out, ou
         for n in range(-3, N_CHUNKS):
             if valid(n + 3):
                 load(n + 3)
+            if valid(n + 2):
+                vector_regroup_x(n + 2)
+            if valid(n + 1):
+                vector_regroup_g(n + 1)
+            if valid(n + 2):
+                vector_negate(n + 2)
             if valid(n):
                 vector_inner(n)
             if valid(n + 2):
-                vector_regroup_x(n + 2)
-            if valid(n):
-                vector_outer(n)
-            if valid(n + 2):
                 vector_clamp(n + 2)
             if valid(n):
-                quantize_basis(n)
-            if valid(n + 1):
-                vector_regroup_g(n + 1)
-            if valid(n):
+                vector_outer(n)
                 quantize_g(n)
+                quantize_basis(n)
             if valid(n + 2):
                 tensor_pass_g(n + 2)
             if valid(n + 1):

@@ -64,21 +64,20 @@ def tile_kanlayer_t_kernel(tc, x, base_weight, spline_weight, grid, grad_out, ou
             held[("g_rows", n)] = g_rows
 
         def vector_regroup_x(n):
-            signed = split.tile([P, CHUNK, 2, FEATURES * PACK], BF16)
+            v = split.tile([P, CHUNK, FEATURES * PACK], BF16)
             nc.vector.tensor_copy(
-                out=signed[:, :, 1, :].rearrange("p c (q r t) -> p c q t r", r=RUN, t=PACK),
+                out=v[:].rearrange("p c (q r t) -> p c q t r", r=RUN, t=PACK),
                 in_=held[("x_rows", n)][:].rearrange("p c t (q r) -> p c q t r", r=RUN),
             )
-            held[("signed", n)] = signed
+            held[("v", n)] = v
 
-        def vector_negate(n):
-            signed = held[("signed", n)]
-            nc.vector.tensor_scalar_mul(out=signed[:, :, 0, :], in0=signed[:, :, 1, :], scalar1=-1.0)
-
-        def vector_clamp(n):
+        def vector_clamp_low(n):
             part = split.tile([P, CHUNK, 2, FEATURES * PACK], BF16)
-            nc.vector.tensor_scalar_max(out=part[:], in0=held[("signed", n)][:], scalar1=0.0)
+            nc.vector.tensor_scalar_min(out=part[:, :, 0, :], in0=held[("v", n)][:], scalar1=0.0)
             held[("part", n)] = part
+
+        def vector_clamp_high(n):
+            nc.vector.tensor_scalar_max(out=held[("part", n)][:, :, 1, :], in0=held[("v", n)][:], scalar1=0.0)
 
         def vector_regroup_g(n):
             g = ready.tile([P, CHUNK, OUTS, PACK], BF16, align_bytes=64)
@@ -105,7 +104,8 @@ def tile_kanlayer_t_kernel(tc, x, base_weight, spline_weight, grid, grad_out, ou
 
         def scalar_work(n):
             far_sq = squares.tile([P, CHUNK, 2, FEATURES * PACK], F32)
-            nc.scalar.activation(out=far_sq[:], in_=held[("signed", n)][:], func=ACT.Square, bias=1.0, scale=1.0)
+            nc.scalar.activation(out=far_sq[:, :, 0, :], in_=held[("v", n)][:], func=ACT.Square, bias=1.0, scale=-1.0)
+            nc.scalar.activation(out=far_sq[:, :, 1, :], in_=held[("v", n)][:], func=ACT.Square, bias=1.0, scale=1.0)
             part_sq = squares.tile([P, CHUNK, 2, FEATURES * PACK], F32)
             nc.scalar.activation(out=part_sq[:], in_=held[("part", n)][:], func=ACT.Square)
             held[("far_sq", n)] = far_sq
@@ -186,11 +186,11 @@ def tile_kanlayer_t_kernel(tc, x, base_weight, spline_weight, grid, grad_out, ou
             if valid(n + 1):
                 vector_regroup_g(n + 1)
             if valid(n + 2):
-                vector_negate(n + 2)
+                vector_clamp_low(n + 2)
             if valid(n):
                 vector_inner(n)
             if valid(n + 2):
-                vector_clamp(n + 2)
+                vector_clamp_high(n + 2)
             if valid(n):
                 vector_outer(n)
                 quantize_g(n)

@@ -22,7 +22,7 @@ COLS = FEATURES * SPLINES
 O_BLOCKS = OUTS // P
 RUN = 4
 
-G_COLS_VECTOR = 76
+G_COLS_VECTOR = 88
 G_COLS_TENSOR = 204
 
 FLOPS = 2 * TOKENS * OUTS * COLS

@@ -16,8 +16,9 @@ TOKENS, FEATURES, OUTS, SPLINES = 16384, 128, 512, 4
 P = 128
 PACK = 4
 K_PASS = P * PACK
-CHUNK = 2
-N_CHUNKS = TOKENS // (K_PASS * CHUNK)
+N_PASSES = TOKENS // K_PASS
+CHUNKS = [1, 1] + [2] * ((N_PASSES - 4) // 2) + [1, 1]
+N_CHUNKS = len(CHUNKS)
 COLS = FEATURES * SPLINES
 O_BLOCKS = OUTS // P
 RUN = 4
@@ -31,8 +32,9 @@ BYTES = TOKENS * FEATURES * 2 + TOKENS * OUTS * 2 + OUTS * COLS * 4
 
 def tile_kanlayer_t_kernel(tc, x, base_weight, spline_weight, grid, grad_out, out):
     nc = tc.nc
-    x_chunks = x.rearrange("(n c p t) i -> n p c (t i)", c=CHUNK, p=P, t=PACK)
-    g_chunks = grad_out.rearrange("(n c p t) o -> n p c (t o)", c=CHUNK, p=P, t=PACK)
+    first_pass = [sum(CHUNKS[:n]) for n in range(N_CHUNKS)]
+    x_passes = x.rearrange("(s p t) i -> p s (t i)", p=P, t=PACK)
+    g_passes = grad_out.rearrange("(s p t) o -> p s (t o)", p=P, t=PACK)
     vector_cols = slice(0, G_COLS_VECTOR)
     tensor_cols = slice(G_COLS_VECTOR, G_COLS_VECTOR + G_COLS_TENSOR)
     scalar_cols = slice(G_COLS_VECTOR + G_COLS_TENSOR, OUTS)
@@ -56,15 +58,16 @@ def tile_kanlayer_t_kernel(tc, x, base_weight, spline_weight, grid, grad_out, ou
         held = {}
 
         def load(n):
-            x_rows = loads.tile([P, CHUNK, PACK, FEATURES], BF16)
-            nc.sync.dma_start(out=x_rows[:].rearrange("p c t i -> p c (t i)"), in_=x_chunks[n])
-            g_rows = loads.tile([P, CHUNK, PACK, OUTS], BF16)
-            nc.sync.dma_start(out=g_rows[:].rearrange("p c t o -> p c (t o)"), in_=g_chunks[n])
+            passes = slice(first_pass[n], first_pass[n] + CHUNKS[n])
+            x_rows = loads.tile([P, CHUNKS[n], PACK, FEATURES], BF16)
+            nc.sync.dma_start(out=x_rows[:].rearrange("p c t i -> p c (t i)"), in_=x_passes[:, passes, :])
+            g_rows = loads.tile([P, CHUNKS[n], PACK, OUTS], BF16)
+            nc.sync.dma_start(out=g_rows[:].rearrange("p c t o -> p c (t o)"), in_=g_passes[:, passes, :])
             held[("x_rows", n)] = x_rows
             held[("g_rows", n)] = g_rows
 
         def vector_regroup_x(n):
-            v = split.tile([P, CHUNK, FEATURES * PACK], BF16)
+            v = split.tile([P, CHUNKS[n], FEATURES * PACK], BF16)
             nc.vector.tensor_copy(
                 out=v[:].rearrange("p c (q r t) -> p c q t r", r=RUN, t=PACK),
                 in_=held[("x_rows", n)][:].rearrange("p c t (q r) -> p c q t r", r=RUN),
@@ -72,7 +75,7 @@ def tile_kanlayer_t_kernel(tc, x, base_weight, spline_weight, grid, grad_out, ou
             held[("v", n)] = v
 
         def vector_clamp_low(n):
-            part = split.tile([P, CHUNK, 2, FEATURES * PACK], BF16)
+            part = split.tile([P, CHUNKS[n], 2, FEATURES * PACK], BF16)
             nc.vector.tensor_scalar_min(out=part[:, :, 0, :], in0=held[("v", n)][:], scalar1=0.0)
             held[("part", n)] = part
 
@@ -80,7 +83,7 @@ def tile_kanlayer_t_kernel(tc, x, base_weight, spline_weight, grid, grad_out, ou
             nc.vector.tensor_scalar_max(out=held[("part", n)][:, :, 1, :], in0=held[("v", n)][:], scalar1=0.0)
 
         def vector_regroup_g(n):
-            g = ready.tile([P, CHUNK, OUTS, PACK], BF16, align_bytes=64)
+            g = ready.tile([P, CHUNKS[n], OUTS, PACK], BF16, align_bytes=64)
             nc.vector.tensor_copy(
                 out=g[:, :, vector_cols, :].rearrange("p c (q r) t -> p c q t r", r=RUN),
                 in_=held[("g_rows", n)][:, :, :, vector_cols].rearrange("p c t (q r) -> p c q t r", r=RUN),
@@ -89,7 +92,7 @@ def tile_kanlayer_t_kernel(tc, x, base_weight, spline_weight, grid, grad_out, ou
 
         def tensor_pass_g(n):
             g_rows = held[("g_rows", n)]
-            for c in range(CHUNK):
+            for c in range(CHUNKS[n]):
                 passed = psum_g.tile([P, G_COLS_TENSOR, PACK], BF16)
                 for half in range(2):
                     half_cols = slice(half * G_COLS_TENSOR // 2, (half + 1) * G_COLS_TENSOR // 2)
@@ -103,16 +106,16 @@ def tile_kanlayer_t_kernel(tc, x, base_weight, spline_weight, grid, grad_out, ou
                 held[("passed", n, c)] = passed
 
         def scalar_work(n):
-            far_sq = squares.tile([P, CHUNK, 2, FEATURES * PACK], F32)
+            far_sq = squares.tile([P, CHUNKS[n], 2, FEATURES * PACK], F32)
             nc.scalar.activation(out=far_sq[:, :, 0, :], in_=held[("v", n)][:], func=ACT.Square, bias=1.0, scale=-1.0)
             nc.scalar.activation(out=far_sq[:, :, 1, :], in_=held[("v", n)][:], func=ACT.Square, bias=1.0, scale=1.0)
-            part_sq = squares.tile([P, CHUNK, 2, FEATURES * PACK], F32)
+            part_sq = squares.tile([P, CHUNKS[n], 2, FEATURES * PACK], F32)
             nc.scalar.activation(out=part_sq[:], in_=held[("part", n)][:], func=ACT.Square)
             held[("far_sq", n)] = far_sq
             held[("part_sq", n)] = part_sq
             g = held[("g", n)]
             g_rows = held[("g_rows", n)]
-            for c in range(CHUNK):
+            for c in range(CHUNKS[n]):
                 nc.scalar.copy(out=g[:, c, tensor_cols, :], in_=held[("passed", n, c)][:])
             nc.scalar.copy(
                 out=g[:, :, scalar_cols, :].rearrange("p c (q r) t -> p c q t r", r=RUN),
@@ -120,7 +123,7 @@ def tile_kanlayer_t_kernel(tc, x, base_weight, spline_weight, grid, grad_out, ou
             )
 
         def vector_inner(n):
-            basis2 = ready.tile([P, CHUNK, SPLINES, FEATURES * PACK], BF16, align_bytes=64)
+            basis2 = ready.tile([P, CHUNKS[n], SPLINES, FEATURES * PACK], BF16, align_bytes=64)
             nc.vector.scalar_tensor_tensor(
                 out=basis2[:, :, 1:3, :].rearrange("p c l w -> p c (l w)"),
                 in0=held[("part_sq", n)][:].rearrange("p c s w -> p c (s w)"),
@@ -137,8 +140,8 @@ def tile_kanlayer_t_kernel(tc, x, base_weight, spline_weight, grid, grad_out, ou
             )
 
         def quantize_basis(n):
-            b_codes = packed.tile([P, CHUNK, COLS], U32, align_bytes=64)
-            b_scales = packed.tile([P, CHUNK, COLS], U8, align_bytes=64)
+            b_codes = packed.tile([P, CHUNKS[n], COLS], U32, align_bytes=64)
+            b_scales = packed.tile([P, CHUNKS[n], COLS], U8, align_bytes=64)
             nc.vector.quantize_mx(
                 out=b_codes[:].rearrange("p c w -> p (c w)").bitcast(E4M3_X4),
                 scales=b_scales[:].rearrange("p c w -> p (c w)"),
@@ -148,8 +151,8 @@ def tile_kanlayer_t_kernel(tc, x, base_weight, spline_weight, grid, grad_out, ou
             held[("b_scales", n)] = b_scales
 
         def quantize_g(n):
-            g_codes = packed.tile([P, CHUNK, OUTS], U32, align_bytes=64)
-            g_scales = packed.tile([P, CHUNK, OUTS], U8, align_bytes=64)
+            g_codes = packed.tile([P, CHUNKS[n], OUTS], U32, align_bytes=64)
+            g_scales = packed.tile([P, CHUNKS[n], OUTS], U8, align_bytes=64)
             nc.vector.quantize_mx(
                 out=g_codes[:].rearrange("p c o -> p (c o)").bitcast(E5M2_X4),
                 scales=g_scales[:].rearrange("p c o -> p (c o)"),
@@ -160,10 +163,7 @@ def tile_kanlayer_t_kernel(tc, x, base_weight, spline_weight, grid, grad_out, ou
 
         def multiply(n):
             last = n == N_CHUNKS - 1
-            order = [(c, ob) for c in range(CHUNK) for ob in range(O_BLOCKS)]
-            if last:
-                order = [(c, ob) for ob in range(O_BLOCKS) for c in range(CHUNK)]
-            for c, ob in order:
+            for c, ob in [(c, ob) for c in range(CHUNKS[n]) for ob in range(O_BLOCKS)]:
                 o_cols = slice(ob * P, (ob + 1) * P)
                 nc.tensor.matmul_mx(
                     out=sums[ob][:],
@@ -172,7 +172,7 @@ def tile_kanlayer_t_kernel(tc, x, base_weight, spline_weight, grid, grad_out, ou
                     rhs=held[("b_codes", n)][:, c, :].bitcast(E4M3_X4),
                     rhs_scale=held[("b_scales", n)][:, c, :],
                     start=(n == 0 and c == 0),
-                    stop=(last and c == CHUNK - 1),
+                    stop=(last and c == CHUNKS[n] - 1),
                 )
 
         def valid(n):

@@ -22,8 +22,9 @@ N_CHUNKS = len(CHUNKS)
 COLS = FEATURES * SPLINES
 O_BLOCKS = OUTS // P
 RUN = 4
+RUN_VECTOR = 8
 
-G_COLS_VECTOR = 88
+G_COLS_VECTOR = 96
 G_COLS_TENSOR = 204
 
 FLOPS = 2 * TOKENS * OUTS * COLS
@@ -69,8 +70,8 @@ def tile_kanlayer_t_kernel(tc, x, base_weight, spline_weight, grid, grad_out, ou
         def vector_regroup_x(n):
             v = split.tile([P, CHUNKS[n], FEATURES * PACK], BF16)
             nc.vector.tensor_copy(
-                out=v[:].rearrange("p c (q r t) -> p c q t r", r=RUN, t=PACK),
-                in_=held[("x_rows", n)][:].rearrange("p c t (q r) -> p c q t r", r=RUN),
+                out=v[:].rearrange("p c (q r t) -> p c q t r", r=RUN_VECTOR, t=PACK),
+                in_=held[("x_rows", n)][:].rearrange("p c t (q r) -> p c q t r", r=RUN_VECTOR),
             )
             held[("v", n)] = v
 
@@ -85,8 +86,8 @@ def tile_kanlayer_t_kernel(tc, x, base_weight, spline_weight, grid, grad_out, ou
         def vector_regroup_g(n):
             g = ready.tile([P, CHUNKS[n], OUTS, PACK], BF16, align_bytes=64)
             nc.vector.tensor_copy(
-                out=g[:, :, vector_cols, :].rearrange("p c (q r) t -> p c q t r", r=RUN),
-                in_=held[("g_rows", n)][:, :, :, vector_cols].rearrange("p c t (q r) -> p c q t r", r=RUN),
+                out=g[:, :, vector_cols, :].rearrange("p c (q r) t -> p c q t r", r=RUN_VECTOR),
+                in_=held[("g_rows", n)][:, :, :, vector_cols].rearrange("p c t (q r) -> p c q t r", r=RUN_VECTOR),
             )
             held[("g", n)] = g
 

@@ -34,6 +34,8 @@ BYTES = TOKENS * FEATURES * 2 + TOKENS * OUTS * 2 + OUTS * COLS * 4
 def tile_kanlayer_t_kernel(tc, x, base_weight, spline_weight, grid, grad_out, out):
     nc = tc.nc
     first_pass = [sum(CHUNKS[:n]) for n in range(N_CHUNKS)]
+    groups = [[0], [1]] + [[n, n + 1] for n in range(2, N_CHUNKS, 2)]
+    group_from = dict([(group[0], group) for group in groups])
     x_passes = x.rearrange("(s p t) i -> p s (t i)", p=P, t=PACK)
     g_passes = grad_out.rearrange("(s p t) o -> p s (t o)", p=P, t=PACK)
     vector_cols = slice(0, G_COLS_VECTOR)
@@ -42,6 +44,7 @@ def tile_kanlayer_t_kernel(tc, x, base_weight, spline_weight, grid, grad_out, ou
 
     with ExitStack() as stack:
         consts = stack.enter_context(tc.tile_pool(name="consts", bufs=1))
+        loads_x = stack.enter_context(tc.tile_pool(name="loads_x", bufs=3))
         loads = stack.enter_context(tc.tile_pool(name="loads", bufs=4))
         split = stack.enter_context(tc.tile_pool(name="split", bufs=3))
         squares = stack.enter_context(tc.tile_pool(name="squares", bufs=3))
@@ -58,30 +61,44 @@ def tile_kanlayer_t_kernel(tc, x, base_weight, spline_weight, grid, grad_out, ou
         stack.enter_context(tc.manual_schedule())
         held = {}
 
-        def load(n):
-            passes = slice(first_pass[n], first_pass[n] + CHUNKS[n])
-            x_rows = loads.tile([P, CHUNKS[n], PACK, FEATURES], BF16)
+        def group_passes(group):
+            return sum([CHUNKS[n] for n in group])
+
+        def load_x(group):
+            passes = slice(first_pass[group[0]], first_pass[group[0]] + group_passes(group))
+            x_rows = loads_x.tile([P, group_passes(group), PACK, FEATURES], BF16)
             nc.sync.dma_start(out=x_rows[:].rearrange("p c t i -> p c (t i)"), in_=x_passes[:, passes, :])
+            held[("x_rows", group[0])] = x_rows
+
+        def load_g(n):
+            passes = slice(first_pass[n], first_pass[n] + CHUNKS[n])
             g_rows = loads.tile([P, CHUNKS[n], PACK, OUTS], BF16)
             nc.sync.dma_start(out=g_rows[:].rearrange("p c t o -> p c (t o)"), in_=g_passes[:, passes, :])
-            held[("x_rows", n)] = x_rows
             held[("g_rows", n)] = g_rows
 
-        def vector_regroup_x(n):
-            v = split.tile([P, CHUNKS[n], FEATURES * PACK], BF16)
+        def vector_regroup_x(group):
+            v = split.tile([P, group_passes(group), FEATURES * PACK], BF16)
             nc.vector.tensor_copy(
                 out=v[:].rearrange("p c (q r t) -> p c q t r", r=RUN_VECTOR, t=PACK),
-                in_=held[("x_rows", n)][:].rearrange("p c t (q r) -> p c q t r", r=RUN_VECTOR),
+                in_=held[("x_rows", group[0])][:].rearrange("p c t (q r) -> p c q t r", r=RUN_VECTOR),
             )
-            held[("v", n)] = v
+            held[("v_group", group[0])] = v
+            for n in group:
+                c0 = first_pass[n] - first_pass[group[0]]
+                held[("v", n)] = v[:, c0 : c0 + CHUNKS[n], :]
 
-        def vector_clamp_low(n):
-            part = split.tile([P, CHUNKS[n], 2, FEATURES * PACK], BF16)
-            nc.vector.tensor_scalar_min(out=part[:, :, 0, :], in0=held[("v", n)][:], scalar1=0.0)
-            held[("part", n)] = part
+        def vector_clamp_low(group):
+            part = split.tile([P, group_passes(group), 2, FEATURES * PACK], BF16)
+            nc.vector.tensor_scalar_min(out=part[:, :, 0, :], in0=held[("v_group", group[0])][:], scalar1=0.0)
+            held[("part_group", group[0])] = part
+            for n in group:
+                c0 = first_pass[n] - first_pass[group[0]]
+                held[("part", n)] = part[:, c0 : c0 + CHUNKS[n], :, :]
 
-        def vector_clamp_high(n):
-            nc.vector.tensor_scalar_max(out=held[("part", n)][:, :, 1, :], in0=held[("v", n)][:], scalar1=0.0)
+        def vector_clamp_high(group):
+            nc.vector.tensor_scalar_max(
+                out=held[("part_group", group[0])][:, :, 1, :], in0=held[("v_group", group[0])][:], scalar1=0.0
+            )
 
         def vector_regroup_g(n):
             g = ready.tile([P, CHUNKS[n], OUTS, PACK], BF16, align_bytes=64)
@@ -108,10 +125,10 @@ def tile_kanlayer_t_kernel(tc, x, base_weight, spline_weight, grid, grad_out, ou
 
         def scalar_work(n):
             far_sq = squares.tile([P, CHUNKS[n], 2, FEATURES * PACK], F32)
-            nc.scalar.activation(out=far_sq[:, :, 0, :], in_=held[("v", n)][:], func=ACT.Square, bias=1.0, scale=-1.0)
-            nc.scalar.activation(out=far_sq[:, :, 1, :], in_=held[("v", n)][:], func=ACT.Square, bias=1.0, scale=1.0)
+            nc.scalar.activation(out=far_sq[:, :, 0, :], in_=held[("v", n)], func=ACT.Square, bias=1.0, scale=-1.0)
+            nc.scalar.activation(out=far_sq[:, :, 1, :], in_=held[("v", n)], func=ACT.Square, bias=1.0, scale=1.0)
             part_sq = squares.tile([P, CHUNKS[n], 2, FEATURES * PACK], F32)
-            nc.scalar.activation(out=part_sq[:], in_=held[("part", n)][:], func=ACT.Square)
+            nc.scalar.activation(out=part_sq[:], in_=held[("part", n)], func=ACT.Square)
             held[("far_sq", n)] = far_sq
             held[("part_sq", n)] = part_sq
             g = held[("g", n)]
@@ -179,19 +196,21 @@ def tile_kanlayer_t_kernel(tc, x, base_weight, spline_weight, grid, grad_out, ou
         def valid(n):
             return 0 <= n < N_CHUNKS
 
-        for n in range(-3, N_CHUNKS):
+        for n in range(-4, N_CHUNKS):
+            if n + 4 in group_from:
+                load_x(group_from[n + 4])
             if valid(n + 3):
-                load(n + 3)
-            if valid(n + 2):
-                vector_regroup_x(n + 2)
+                load_g(n + 3)
+            if n + 2 in group_from:
+                vector_regroup_x(group_from[n + 2])
             if valid(n + 1):
                 vector_regroup_g(n + 1)
-            if valid(n + 2):
-                vector_clamp_low(n + 2)
+            if n + 2 in group_from:
+                vector_clamp_low(group_from[n + 2])
             if valid(n):
                 vector_inner(n)
-            if valid(n + 2):
-                vector_clamp_high(n + 2)
+            if n + 2 in group_from:
+                vector_clamp_high(group_from[n + 2])
             if valid(n):
                 vector_outer(n)
                 quantize_g(n)

@@ -24,7 +24,7 @@ O_BLOCKS = OUTS // P
 RUN = 4
 RUN_VECTOR = 8
 
-G_COLS_VECTOR = 96
+G_COLS_VECTOR = 192
 G_COLS_TENSOR = 204
 
 FLOPS = 2 * TOKENS * OUTS * COLS
@@ -68,7 +68,11 @@ def tile_kanlayer_t_kernel(tc, x, base_weight, spline_weight, grid, grad_out, ou
             passes = slice(first_pass[group[0]], first_pass[group[0]] + group_passes(group))
             x_rows = loads_x.tile([P, group_passes(group), PACK, FEATURES], BF16)
             nc.sync.dma_start(out=x_rows[:].rearrange("p c t i -> p c (t i)"), in_=x_passes[:, passes, :])
-            held[("x_rows", group[0])] = x_rows
+            v = x_rows[:].rearrange("p c t i -> p c (t i)")
+            held[("v_group", group[0])] = v
+            for n in group:
+                c0 = first_pass[n] - first_pass[group[0]]
+                held[("v", n)] = v[:, c0 : c0 + CHUNKS[n], :]
 
         def load_g(n):
             passes = slice(first_pass[n], first_pass[n] + CHUNKS[n])
@@ -76,20 +80,9 @@ def tile_kanlayer_t_kernel(tc, x, base_weight, spline_weight, grid, grad_out, ou
             nc.sync.dma_start(out=g_rows[:].rearrange("p c t o -> p c (t o)"), in_=g_passes[:, passes, :])
             held[("g_rows", n)] = g_rows
 
-        def vector_regroup_x(group):
-            v = split.tile([P, group_passes(group), FEATURES * PACK], BF16)
-            nc.vector.tensor_copy(
-                out=v[:].rearrange("p c (q r t) -> p c q t r", r=RUN_VECTOR, t=PACK),
-                in_=held[("x_rows", group[0])][:].rearrange("p c t (q r) -> p c q t r", r=RUN_VECTOR),
-            )
-            held[("v_group", group[0])] = v
-            for n in group:
-                c0 = first_pass[n] - first_pass[group[0]]
-                held[("v", n)] = v[:, c0 : c0 + CHUNKS[n], :]
-
         def vector_clamp_low(group):
             part = split.tile([P, group_passes(group), 2, FEATURES * PACK], BF16)
-            nc.vector.tensor_scalar_min(out=part[:, :, 0, :], in0=held[("v_group", group[0])][:], scalar1=0.0)
+            nc.vector.tensor_scalar_min(out=part[:, :, 0, :], in0=held[("v_group", group[0])], scalar1=0.0)
             held[("part_group", group[0])] = part
             for n in group:
                 c0 = first_pass[n] - first_pass[group[0]]
@@ -97,7 +90,7 @@ def tile_kanlayer_t_kernel(tc, x, base_weight, spline_weight, grid, grad_out, ou
 
         def vector_clamp_high(group):
             nc.vector.tensor_scalar_max(
-                out=held[("part_group", group[0])][:, :, 1, :], in0=held[("v_group", group[0])][:], scalar1=0.0
+                out=held[("part_group", group[0])][:, :, 1, :], in0=held[("v_group", group[0])], scalar1=0.0
             )
 
         def vector_regroup_g(n):
@@ -125,10 +118,20 @@ def tile_kanlayer_t_kernel(tc, x, base_weight, spline_weight, grid, grad_out, ou
 
         def scalar_work(n):
             far_sq = squares.tile([P, CHUNKS[n], 2, FEATURES * PACK], F32)
-            nc.scalar.activation(out=far_sq[:, :, 0, :], in_=held[("v", n)], func=ACT.Square, bias=1.0, scale=-1.0)
-            nc.scalar.activation(out=far_sq[:, :, 1, :], in_=held[("v", n)], func=ACT.Square, bias=1.0, scale=1.0)
+            for side, sign in ((0, -1.0), (1, 1.0)):
+                nc.scalar.activation(
+                    out=far_sq[:, :, side, :].rearrange("p c (i t) -> p c i t", t=PACK),
+                    in_=held[("v", n)].rearrange("p c (t i) -> p c i t", t=PACK),
+                    func=ACT.Square,
+                    bias=1.0,
+                    scale=sign,
+                )
             part_sq = squares.tile([P, CHUNKS[n], 2, FEATURES * PACK], F32)
-            nc.scalar.activation(out=part_sq[:], in_=held[("part", n)], func=ACT.Square)
+            nc.scalar.activation(
+                out=part_sq[:].rearrange("p c s (i t) -> p (c s) i t", t=PACK),
+                in_=held[("part", n)].rearrange("p c s (t i) -> p (c s) i t", t=PACK),
+                func=ACT.Square,
+            )
             held[("far_sq", n)] = far_sq
             held[("part_sq", n)] = part_sq
             g = held[("g", n)]
@@ -201,8 +204,6 @@ def tile_kanlayer_t_kernel(tc, x, base_weight, spline_weight, grid, grad_out, ou
                 load_x(group_from[n + 4])
             if valid(n + 3):
                 load_g(n + 3)
-            if n + 2 in group_from:
-                vector_regroup_x(group_from[n + 2])
             if valid(n + 1):
                 vector_regroup_g(n + 1)
             if n + 2 in group_from:

from contextlib import ExitStack

import concourse.masks as masks
import concourse.mybir as mybir

BF16 = mybir.dt.bfloat16
F32 = mybir.dt.float32
U32 = mybir.dt.uint32
U8 = mybir.dt.uint8
E4M3_X4 = mybir.dt.float8_e4m3fn_x4
E5M2_X4 = mybir.dt.float8_e5m2_x4
ALU = mybir.AluOpType
ACT = mybir.ActivationFunctionType

TOKENS, FEATURES, OUTS, SPLINES = 16384, 128, 512, 4
P = 128
PACK = 4
K_PASS = P * PACK
N_PASSES = TOKENS // K_PASS
CHUNKS = [1, 1] + [2] * ((N_PASSES - 4) // 2) + [1, 1]
N_CHUNKS = len(CHUNKS)
COLS = FEATURES * SPLINES
O_BLOCKS = OUTS // P
RUN = 4
RUN_VECTOR = 8

G_COLS_VECTOR = 192
G_COLS_TENSOR = 204

FLOPS = 2 * TOKENS * OUTS * COLS
BYTES = TOKENS * FEATURES * 2 + TOKENS * OUTS * 2 + OUTS * COLS * 4


def tile_kanlayer_t_kernel(tc, x, base_weight, spline_weight, grid, grad_out, out):
    nc = tc.nc
    first_pass = [sum(CHUNKS[:n]) for n in range(N_CHUNKS)]
    groups = [[0], [1]] + [[n, n + 1] for n in range(2, N_CHUNKS, 2)]
    group_from = dict([(group[0], group) for group in groups])
    x_passes = x.rearrange("(s p t) i -> p s (t i)", p=P, t=PACK)
    g_passes = grad_out.rearrange("(s p t) o -> p s (t o)", p=P, t=PACK)
    vector_cols = slice(0, G_COLS_VECTOR)
    tensor_cols = slice(G_COLS_VECTOR, G_COLS_VECTOR + G_COLS_TENSOR)
    scalar_cols = slice(G_COLS_VECTOR + G_COLS_TENSOR, OUTS)

    with ExitStack() as stack:
        consts = stack.enter_context(tc.tile_pool(name="consts", bufs=1))
        loads_x = stack.enter_context(tc.tile_pool(name="loads_x", bufs=3))
        loads = stack.enter_context(tc.tile_pool(name="loads", bufs=4))
        split = stack.enter_context(tc.tile_pool(name="split", bufs=3))
        squares = stack.enter_context(tc.tile_pool(name="squares", bufs=3))
        ready = stack.enter_context(tc.tile_pool(name="ready", bufs=3))
        packed = stack.enter_context(tc.tile_pool(name="packed", bufs=3))
        results = stack.enter_context(tc.tile_pool(name="results", bufs=4))
        psum = stack.enter_context(tc.psum_pool(name="psum", bufs=1))
        psum_g = stack.enter_context(tc.psum_pool(name="psum_g", bufs=4))

        identity = consts.tile([P, P], BF16)
        masks.make_identity(nc, identity[:])
        sums = [psum.tile([P, COLS], F32, name="sums%d" % ob) for ob in range(O_BLOCKS)]

        stack.enter_context(tc.manual_schedule())
        held = {}

        def group_passes(group):
            return sum([CHUNKS[n] for n in group])

        def load_x(group):
            passes = slice(first_pass[group[0]], first_pass[group[0]] + group_passes(group))
            x_rows = loads_x.tile([P, group_passes(group), PACK, FEATURES], BF16)
            nc.sync.dma_start(out=x_rows[:].rearrange("p c t i -> p c (t i)"), in_=x_passes[:, passes, :])
            v = x_rows[:].rearrange("p c t i -> p c (t i)")
            held[("v_group", group[0])] = v
            for n in group:
                c0 = first_pass[n] - first_pass[group[0]]
                held[("v", n)] = v[:, c0 : c0 + CHUNKS[n], :]

        def load_g(n):
            passes = slice(first_pass[n], first_pass[n] + CHUNKS[n])
            g_rows = loads.tile([P, CHUNKS[n], PACK, OUTS], BF16)
            nc.sync.dma_start(out=g_rows[:].rearrange("p c t o -> p c (t o)"), in_=g_passes[:, passes, :])
            held[("g_rows", n)] = g_rows

        def vector_clamp_low(group):
            part = split.tile([P, group_passes(group), 2, FEATURES * PACK], BF16)
            nc.vector.tensor_scalar_min(out=part[:, :, 0, :], in0=held[("v_group", group[0])], scalar1=0.0)
            held[("part_group", group[0])] = part
            for n in group:
                c0 = first_pass[n] - first_pass[group[0]]
                held[("part", n)] = part[:, c0 : c0 + CHUNKS[n], :, :]

        def vector_clamp_high(group):
            nc.vector.tensor_scalar_max(
                out=held[("part_group", group[0])][:, :, 1, :], in0=held[("v_group", group[0])], scalar1=0.0
            )

        def vector_regroup_g(n):
            g = ready.tile([P, CHUNKS[n], OUTS, PACK], BF16, align_bytes=64)
            nc.vector.tensor_copy(
                out=g[:, :, vector_cols, :].rearrange("p c (q r) t -> p c q t r", r=RUN_VECTOR),
                in_=held[("g_rows", n)][:, :, :, vector_cols].rearrange("p c t (q r) -> p c q t r", r=RUN_VECTOR),
            )
            held[("g", n)] = g

        def tensor_pass_g(n):
            g_rows = held[("g_rows", n)]
            for c in range(CHUNKS[n]):
                passed = psum_g.tile([P, G_COLS_TENSOR, PACK], BF16)
                for half in range(2):
                    half_cols = slice(half * G_COLS_TENSOR // 2, (half + 1) * G_COLS_TENSOR // 2)
                    nc.tensor.matmul(
                        out=passed[:, half_cols, :].rearrange("p o t -> p t o"),
                        lhsT=identity[:],
                        rhs=g_rows[:, c, :, tensor_cols][:, :, half_cols],
                        start=True,
                        stop=True,
                    )
                held[("passed", n, c)] = passed

        def scalar_work(n):
            far_sq = squares.tile([P, CHUNKS[n], 2, FEATURES * PACK], F32)
            for side, sign in ((0, -1.0), (1, 1.0)):
                nc.scalar.activation(
                    out=far_sq[:, :, side, :].rearrange("p c (i t) -> p c i t", t=PACK),
                    in_=held[("v", n)].rearrange("p c (t i) -> p c i t", t=PACK),
                    func=ACT.Square,
                    bias=1.0,
                    scale=sign,
                )
            part_sq = squares.tile([P, CHUNKS[n], 2, FEATURES * PACK], F32)
            nc.scalar.activation(
                out=part_sq[:].rearrange("p c s (i t) -> p (c s) i t", t=PACK),
                in_=held[("part", n)].rearrange("p c s (t i) -> p (c s) i t", t=PACK),
                func=ACT.Square,
            )
            held[("far_sq", n)] = far_sq
            held[("part_sq", n)] = part_sq
            g = held[("g", n)]
            g_rows = held[("g_rows", n)]
            for c in range(CHUNKS[n]):
                nc.scalar.copy(out=g[:, c, tensor_cols, :], in_=held[("passed", n, c)][:])
            nc.scalar.copy(
                out=g[:, :, scalar_cols, :].rearrange("p c (q r) t -> p c q t r", r=RUN),
                in_=g_rows[:, :, :, scalar_cols].rearrange("p c t (q r) -> p c q t r", r=RUN),
            )

        def vector_inner(n):
            basis2 = ready.tile([P, CHUNKS[n], SPLINES, FEATURES * PACK], BF16, align_bytes=64)
            nc.vector.scalar_tensor_tensor(
                out=basis2[:, :, 1:3, :].rearrange("p c l w -> p c (l w)"),
                in0=held[("part_sq", n)][:].rearrange("p c s w -> p c (s w)"),
                scalar=-3.0,
                in1=held[("far_sq", n)][:].rearrange("p c s w -> p c (s w)"),
                op0=ALU.mult,
                op1=ALU.add,
            )
            held[("basis2", n)] = basis2

        def vector_outer(n):
            nc.vector.tensor_copy(
                out=held[("basis2", n)][:, :, 0 : SPLINES : SPLINES - 1, :], in_=held[("part_sq", n)][:]
            )

        def quantize_basis(n):
            b_codes = packed.tile([P, CHUNKS[n], COLS], U32, align_bytes=64)
            b_scales = packed.tile([P, CHUNKS[n], COLS], U8, align_bytes=64)
            nc.vector.quantize_mx(
                out=b_codes[:].rearrange("p c w -> p (c w)").bitcast(E4M3_X4),
                scales=b_scales[:].rearrange("p c w -> p (c w)"),
                in_=held[("basis2", n)][:].rearrange("p c l w -> p (c l w)"),
            )
            held[("b_codes", n)] = b_codes
            held[("b_scales", n)] = b_scales

        def quantize_g(n):
            g_codes = packed.tile([P, CHUNKS[n], OUTS], U32, align_bytes=64)
            g_scales = packed.tile([P, CHUNKS[n], OUTS], U8, align_bytes=64)
            nc.vector.quantize_mx(
                out=g_codes[:].rearrange("p c o -> p (c o)").bitcast(E5M2_X4),
                scales=g_scales[:].rearrange("p c o -> p (c o)"),
                in_=held[("g", n)][:].rearrange("p c o t -> p (c o t)"),
            )
            held[("g_codes", n)] = g_codes
            held[("g_scales", n)] = g_scales

        def multiply(n):
            last = n == N_CHUNKS - 1
            for c, ob in [(c, ob) for c in range(CHUNKS[n]) for ob in range(O_BLOCKS)]:
                o_cols = slice(ob * P, (ob + 1) * P)
                nc.tensor.matmul_mx(
                    out=sums[ob][:],
                    lhsT=held[("g_codes", n)][:, c, o_cols].bitcast(E5M2_X4),
                    lhsT_scale=held[("g_scales", n)][:, c, o_cols],
                    rhs=held[("b_codes", n)][:, c, :].bitcast(E4M3_X4),
                    rhs_scale=held[("b_scales", n)][:, c, :],
                    start=(n == 0 and c == 0),
                    stop=(last and c == CHUNKS[n] - 1),
                )

        def valid(n):
            return 0 <= n < N_CHUNKS

        for n in range(-4, N_CHUNKS):
            if n + 4 in group_from:
                load_x(group_from[n + 4])
            if valid(n + 3):
                load_g(n + 3)
            if valid(n + 1):
                vector_regroup_g(n + 1)
            if n + 2 in group_from:
                vector_clamp_low(group_from[n + 2])
            if valid(n):
                vector_inner(n)
            if n + 2 in group_from:
                vector_clamp_high(group_from[n + 2])
            if valid(n):
                vector_outer(n)
                quantize_g(n)
                quantize_basis(n)
            if valid(n + 2):
                tensor_pass_g(n + 2)
            if valid(n + 1):
                scalar_work(n + 1)
            if valid(n):
                multiply(n)

        for ob in range(O_BLOCKS):
            result = results.tile([P, FEATURES, SPLINES], F32)
            columns = sums[ob][:].rearrange("p (l i) -> p i l", l=SPLINES)
            if ob % 2 == 0:
                nc.vector.tensor_scalar_mul(out=result[:], in0=columns, scalar1=0.5)
            else:
                nc.scalar.mul(out=result[:], in_=columns, mul=0.5)
            nc.sync.dma_start(out=out[ob * P : (ob + 1) * P], in_=result[:])
